import numpy as np
import ml_dtypes


def mxq(x, axis, fmt="e4m3"):
    dtype, down = {"e4m3": (ml_dtypes.float8_e4m3fn, 7), "e5m2": (ml_dtypes.float8_e5m2, 14)}[fmt]
    v = np.moveaxis(np.asarray(x, np.float32).astype(ml_dtypes.bfloat16).astype(np.float64), axis, -1)
    blocks = v.reshape(v.shape[:-1] + (-1, 32))
    amax = np.abs(blocks).max(-1, keepdims=True)
    byte = np.maximum(np.where(amax > 0, np.frexp(amax)[1] - 1 + 127, 0) - down, 1)
    scale = np.exp2(byte - 127.0)
    codes = (blocks / scale).astype(np.float32).astype(dtype).astype(np.float64)
    return np.moveaxis((codes * scale).reshape(v.shape), -1, axis)


WIDE = False


def mx_kscale(k):
    if not WIDE:
        return np.ones(k)
    levels = np.array([10, -10, 5, -5, 0])
    a = np.random.permutation(np.resize(levels, k // 512 * 4)).reshape(k // 512, 4)
    idx = np.arange(k)
    return np.exp2(a[idx // 512, idx % 128 // 32])


BF16 = ml_dtypes.bfloat16


def bf(x):
    return np.asarray(x, np.float32).astype(BF16)


def f64(x):
    return np.asarray(x).astype(np.float64)


E2M1 = np.array([0.0, 0.5, 1.0, 1.5, 2.0, 3.0, 4.0, 6.0, -0.0, -0.5, -1.0, -1.5, -2.0, -3.0, -4.0, -6.0])


def pack_weight(w, fmt):
    k, n = w.shape
    w = f64(bf(w)).reshape(k // 32, 32, n)
    amax = np.abs(w).max(1)
    if fmt == "e4m3":
        byte = np.frexp(amax)[1] - 1 + 127 - 7
    else:
        mant, ex = np.frexp(amax / 6.0)
        byte = np.where(mant > 0.5, ex, ex - 1) + 127
    byte = np.clip(np.where(amax > 0, byte, 1), 1, 254)
    scaled = (w * np.exp2(127.0 - byte)[:, None, :]).reshape(k, n).astype(np.float32)
    by_word = np.ascontiguousarray(scaled.reshape(k // 512, 128, 4, n).transpose(0, 1, 3, 2))
    if fmt == "e4m3":
        words = by_word.astype(ml_dtypes.float8_e4m3fn).view(np.uint8)
    else:
        c = by_word.astype(ml_dtypes.float4_e2m1fn).view(np.uint8) & 0xF
        words = c[..., 0::2] | (c[..., 1::2] << 4)
    return np.ascontiguousarray(words), np.ascontiguousarray(byte.astype(np.uint8).reshape(k // 512, 16, n))


def unpack_weight(words, scales, fmt):
    g, p, n, _ = words.shape
    if fmt == "e4m3":
        vals = np.ascontiguousarray(words).view(ml_dtypes.float8_e4m3fn).astype(np.float64)
    else:
        nib = np.empty((g, p, n, 4), np.uint8)
        nib[..., 0::2] = words & 0xF
        nib[..., 1::2] = words >> 4
        vals = E2M1[nib]
    vals = vals * np.repeat(np.exp2(scales.astype(np.float64) - 127.0), 8, axis=1)[..., None]
    return vals.transpose(0, 1, 3, 2).reshape(g * 512, n)


B, IN, OUT = 4096, 512, 512
G = 3 * OUT
FMT = "e4m3"


def sigmoid(v):
    return 1.0 / (1.0 + np.exp(-v))


def setup_inputs():
    s = mx_kscale(OUT)
    xg = bf(np.random.standard_normal((B, G)) * 0.75)
    hx = bf(np.random.standard_normal((B, OUT)) * s)
    cx = bf(np.random.standard_normal((B, OUT)))
    td0 = bf(np.random.uniform(0.0, 1.0, B))
    td1 = bf(np.random.uniform(0.0, 1.0, B))
    w_hh = np.random.standard_normal((G, OUT)) * 0.7 / np.sqrt(OUT) / s
    w_pi = np.random.standard_normal((OUT, OUT)) * 0.7 / np.sqrt(OUT)
    w_pf = np.random.standard_normal((OUT, OUT)) * 0.7 / np.sqrt(OUT)
    b_hh = bf(np.random.standard_normal(G) * 0.3)
    a = bf(1.0 + 0.1 * np.random.standard_normal(1))
    b = bf(0.5 + 0.1 * np.random.standard_normal(1))
    w_hh_words, w_hh_scales = pack_weight(np.ascontiguousarray(w_hh.T), FMT)
    w_pi_words, w_pi_scales = pack_weight(np.ascontiguousarray(w_pi.T), FMT)
    w_pf_words, w_pf_scales = pack_weight(np.ascontiguousarray(w_pf.T), FMT)
    return {
        "xg": xg,
        "hx": hx,
        "cx": cx,
        "td0": td0,
        "td1": td1,
        "w_hh_words": w_hh_words,
        "w_hh_scales": w_hh_scales,
        "w_pi_words": w_pi_words,
        "w_pi_scales": w_pi_scales,
        "w_pf_words": w_pf_words,
        "w_pf_scales": w_pf_scales,
        "b_hh": b_hh,
        "a": a,
        "b": b,
    }


def reference(xg, hx, cx, td0, td1, w_hh_words, w_hh_scales, w_pi_words, w_pi_scales, w_pf_words, w_pf_scales, b_hh, a, b):
    c = f64(cx)
    cq = mxq(c, 1, "e4m3")
    gates = f64(xg) + (mxq(f64(hx), 1, "e4m3") @ unpack_weight(w_hh_words, w_hh_scales, FMT)) + f64(b_hh)
    i_g, f_g, g_g = np.split(gates, 3, axis=1)
    i_g = sigmoid(i_g + (cq @ unpack_weight(w_pi_words, w_pi_scales, FMT)))
    f_g = sigmoid(f_g + (cq @ unpack_weight(w_pf_words, w_pf_scales, FMT)))
    g_g = np.tanh(g_g)
    forcoff = (f64(a) * np.exp(-f64(b) * f64(td0)))[:, None]
    incoff = (f64(a) * np.exp(-f64(b) * f64(td1)))[:, None]
    f_g = forcoff * f_g
    i_g = incoff * i_g
    return f_g * c + i_g * g_g

@@ -1,0 +1,262 @@
+from contextlib import ExitStack
+
+import concourse.mybir as mybir
+from concourse.masks import make_identity
+
+F32 = mybir.dt.float32
+BF16 = mybir.dt.bfloat16
+I32 = mybir.dt.int32
+U32 = mybir.dt.uint32
+U8 = mybir.dt.uint8
+FP8X4 = mybir.dt.float8_e4m3fn_x4
+ACT = mybir.ActivationFunctionType
+ALU = mybir.AluOpType
+
+P = 128
+ROWS = 4096
+HID = 512
+GATES = 3
+PEEPHOLES = 2
+TILES = ROWS // P
+PAIR = 2
+PAIRS = TILES // PAIR
+WORDS = HID // 2
+W_COLS = (GATES + PEEPHOLES) * HID
+AHEAD = 3
+
+FLOPS = 2 * ROWS * HID * W_COLS
+
+
+def tile_ircnn_lstmcell_pa_t_kernel(
+    tc,
+    xg,
+    hx,
+    cx,
+    td0,
+    td1,
+    w_hh_words,
+    w_hh_scales,
+    w_pi_words,
+    w_pi_scales,
+    w_pf_words,
+    w_pf_scales,
+    b_hh,
+    a,
+    b,
+    out,
+):
+    nc = tc.nc
+
+    xg_v = xg.rearrange("(p t) c -> p t c", t=TILES)
+    hx_v = hx.rearrange("(p t) c -> p t c", t=TILES)
+    cx_v = cx.rearrange("(p t) c -> p t c", t=TILES)
+    out_v = out.rearrange("(p t) c -> p t c", t=TILES)
+
+    with ExitStack() as ctx:
+        const = ctx.enter_context(tc.tile_pool(name="const", bufs=1))
+        loads = ctx.enter_context(tc.tile_pool(name="loads", bufs=1))
+        work = ctx.enter_context(tc.tile_pool(name="work", bufs=1))
+        psum_bias = ctx.enter_context(tc.psum_pool(name="psum_bias", bufs=1))
+        psum_xt = ctx.enter_context(tc.psum_pool(name="psum_xt", bufs=1))
+        psum_acc = ctx.enter_context(tc.psum_pool(name="psum_acc", bufs=4))
+        ctx.enter_context(tc.manual_schedule())
+
+        w_codes = const.tile([P, W_COLS], U32, align_bytes=64)
+        w_scales = const.tile([P, W_COLS], U8, align_bytes=64)
+        nc.vector.memset(w_scales[:].bitcast(I32), 0)
+        weights = (
+            (w_hh_words, w_hh_scales, 0, GATES * HID),
+            (w_pi_words, w_pi_scales, GATES * HID, HID),
+            (w_pf_words, w_pf_scales, GATES * HID + HID, HID),
+        )
+
+        xg_sb = {}
+        hx_sb = {}
+        cx_sb = {}
+
+        def load(pair):
+            rows = slice(pair * PAIR, (pair + 1) * PAIR)
+            hx_pair = loads.tile([P, PAIR, HID], BF16, bufs=AHEAD + 1)
+            nc.sync.dma_start(out=hx_pair[:], in_=hx_v[:, rows, :])
+            cx_pair = loads.tile([P, PAIR, HID], BF16, bufs=AHEAD + 3)
+            nc.sync.dma_start(out=cx_pair[:], in_=cx_v[:, rows, :])
+            xg_pair = loads.tile([P, PAIR, GATES * HID], BF16, bufs=AHEAD + 2)
+            nc.sync.dma_start(out=xg_pair[:], in_=xg_v[:, rows, :])
+            hx_sb[pair] = hx_pair
+            cx_sb[pair] = cx_pair
+            xg_sb[pair] = xg_pair
+
+        load(0)
+        for words, scale_rows, first, width in weights:
+            for quad in range(4):
+                nc.sync.dma_start(
+                    out=w_scales[32 * quad : 32 * quad + 4, first : first + width].bitcast(I32),
+                    in_=scale_rows[0, 4 * quad : 4 * quad + 4, :].bitcast(I32),
+                )
+        for words, scale_rows, first, width in weights:
+            nc.sync.dma_start(
+                out=w_codes[:, first : first + width].bitcast(I32),
+                in_=words[0].rearrange("p n t -> p (n t)").bitcast(I32),
+            )
+
+        ident = const.tile([P, P], F32)
+        make_identity(nc, ident[:])
+
+        bias_row = const.tile([P, GATES * HID], BF16)
+        nc.vector.memset(bias_row[:], 0.0)
+        nc.scalar.dma_start(out=bias_row[0:1, :], in_=b_hh.rearrange("(o c) -> o c", o=1))
+        ones = const.tile([P, P], BF16)
+        nc.vector.memset(ones[:], 1.0)
+        bias_bank = []
+        for gate in range(GATES):
+            bank = psum_bias.tile([P, HID], F32, name="bias_bank%d" % gate)
+            nc.tensor.matmul(
+                out=bank[:],
+                lhsT=ones[:],
+                rhs=bias_row[:, gate * HID : (gate + 1) * HID],
+                start=True,
+                stop=True,
+            )
+            bias_bank.append(bank)
+
+        a_bf = const.tile([P, 1], BF16)
+        nc.scalar.dma_start(out=a_bf[:], in_=a.partition_broadcast(P))
+        b_bf = const.tile([P, 1], BF16)
+        nc.scalar.dma_start(out=b_bf[:], in_=b.partition_broadcast(P))
+        td_sb = const.tile([P, 2, TILES], BF16)
+        nc.scalar.dma_start(out=td_sb[:, 0, :], in_=td0.rearrange("(p t) -> p t", t=TILES))
+        nc.scalar.dma_start(out=td_sb[:, 1, :], in_=td1.rearrange("(p t) -> p t", t=TILES))
+        a_f32 = const.tile([P, 1], F32)
+        nc.vector.tensor_copy(out=a_f32[:], in_=a_bf[:])
+        minus_b = const.tile([P, 1], F32)
+        nc.vector.tensor_scalar_mul(out=minus_b[:], in0=b_bf[:], scalar1=-1.0)
+        decay = const.tile([P, 2, TILES], F32)
+        nc.scalar.activation(out=decay[:], in_=td_sb[:], func=ACT.Exp, scale=minus_b[:, 0:1])
+        nc.vector.tensor_scalar_mul(out=decay[:], in0=decay[:], scalar1=a_f32[:, 0:1])
+
+        xt_bank = {}
+        grouped = {}
+        x_codes = {}
+        x_scales = {}
+        acc = {}
+        gates_sb = {}
+        cx_scaled = {}
+
+        def transpose(t):
+            xt = psum_xt.tile([P, 2, 2, P], F32)
+            for which, src in enumerate((hx_sb, cx_sb)):
+                row_words = src[t // PAIR][:, t % PAIR, :].bitcast(F32)
+                for u in range(2):
+                    nc.tensor.transpose(xt[:, which, u, :], row_words[:, u:WORDS:2], ident[:])
+            xt_bank[t] = xt
+
+        def regroup(t):
+            quads = work.tile([P, 2 * P * 4], BF16, align_bytes=64, bufs=3)
+            nc.scalar.copy(
+                out=quads[:].bitcast(F32).rearrange("p (w r u) -> p w r u", w=2, u=2),
+                in_=xt_bank[t][:].rearrange("p w u r -> p w r u"),
+            )
+            grouped[t] = quads
+
+        def quantise(t):
+            codes = work.tile([P, 2 * P], U32, align_bytes=64, bufs=3)
+            plane = work.tile([P, 2 * P], U8, align_bytes=64, bufs=3)
+            nc.vector.quantize_mx(out=codes[:].bitcast(FP8X4), scales=plane[:], in_=grouped[t][:])
+            x_codes[t] = codes
+            x_scales[t] = plane
+
+        def mx_pass(bank, t, which, w_first, start, stop):
+            rows = slice(which * P, (which + 1) * P)
+            cols = slice(w_first, w_first + HID)
+            nc.tensor.matmul_mx(
+                out=bank[:],
+                lhsT=x_codes[t][:, rows].bitcast(FP8X4),
+                lhsT_scale=x_scales[t][:, rows],
+                rhs=w_codes[:, cols].bitcast(FP8X4),
+                rhs_scale=w_scales[:, cols],
+                start=start,
+                stop=stop,
+            )
+
+        def matmuls(t):
+            for gate in range(GATES):
+                bank = psum_acc.tile([P, HID], F32)
+                peephole = gate < PEEPHOLES
+                mx_pass(bank, t, 0, gate * HID, True, not peephole)
+                if peephole:
+                    mx_pass(bank, t, 1, (GATES + gate) * HID, False, True)
+                acc[(t, gate)] = bank
+
+        def add_bias(t):
+            if t % PAIR == 0:
+                gates_pair = work.tile([P, PAIR, GATES * HID], F32, bufs=4)
+                gates_sb[t // PAIR] = gates_pair
+            for gate in range(GATES):
+                cols = slice(gate * HID, (gate + 1) * HID)
+                nc.vector.tensor_tensor(
+                    out=gates_sb[t // PAIR][:, t % PAIR, cols],
+                    in0=xg_sb[t // PAIR][:, t % PAIR, cols],
+                    in1=bias_bank[gate][:],
+                    op=ALU.add,
+                )
+
+        def add_products(t):
+            for gate in range(GATES):
+                cols = slice(gate * HID, (gate + 1) * HID)
+                nc.vector.tensor_tensor(
+                    out=gates_sb[t // PAIR][:, t % PAIR, cols],
+                    in0=acc[(t, gate)][:],
+                    in1=gates_sb[t // PAIR][:, t % PAIR, cols],
+                    op=ALU.add,
+                )
+
+        def activate(t):
+            if t % PAIR == 0:
+                scaled_pair = work.tile([P, PAIR, HID], F32, bufs=3)
+                cx_scaled[t // PAIR] = scaled_pair
+            mine = gates_sb[t // PAIR][:, t % PAIR, :]
+            nc.scalar.activation(
+                out=cx_scaled[t // PAIR][:, t % PAIR, :],
+                in_=cx_sb[t // PAIR][:, t % PAIR, :],
+                func=ACT.Copy,
+                scale=decay[:, 0, t : t + 1],
+            )
+            nc.scalar.activation(out=mine[:, 0 : 2 * HID], in_=mine[:, 0 : 2 * HID], func=ACT.Sigmoid)
+            nc.scalar.activation(out=mine[:, 2 * HID :], in_=mine[:, 2 * HID :], func=ACT.Tanh)
+            nc.scalar.activation(
+                out=mine[:, 2 * HID :], in_=mine[:, 2 * HID :], func=ACT.Copy, scale=decay[:, 1, t : t + 1]
+            )
+
+        def combine(pair):
+            acts = gates_sb[pair]
+            i_g = acts[:, :, 0:HID]
+            f_g = acts[:, :, HID : 2 * HID]
+            g_g = acts[:, :, 2 * HID :]
+            new_c = work.tile([P, PAIR, HID], F32, bufs=3)
+            nc.gpsimd.tensor_tensor(out=f_g, in0=f_g, in1=cx_scaled[pair][:], op=ALU.mult)
+            nc.gpsimd.tensor_tensor(out=i_g, in0=i_g, in1=g_g, op=ALU.mult)
+            nc.gpsimd.tensor_tensor(out=new_c[:], in0=i_g, in1=f_g, op=ALU.add)
+            nc.sync.dma_start(out=out_v[:, pair * PAIR : (pair + 1) * PAIR, :], in_=new_c[:])
+
+        def live(t):
+            return 0 <= t < TILES
+
+        for t in range(-PAIR * (AHEAD - 1), TILES + PAIR):
+            if t % PAIR == 0 and 1 <= t // PAIR + AHEAD < PAIRS:
+                load(t // PAIR + AHEAD)
+            if live(t + 2):
+                regroup(t + 2)
+            if live(t):
+                add_products(t)
+            if live(t + 1):
+                matmuls(t + 1)
+            if live(t + 3):
+                transpose(t + 3)
+            if live(t):
+                activate(t)
+            if live(t + 1):
+                add_bias(t + 1)
+            if live(t + 2):
+                quantise(t + 2)
+            if t % PAIR == 0 and live(t - PAIR):
+                combine((t - PAIR) // PAIR)

@@ -22,7 +22,9 @@ PAIR = 2
 PAIRS = TILES // PAIR
 WORDS = HID // 2
 W_COLS = (GATES + PEEPHOLES) * HID
-AHEAD = 3
+BATCH = 4
+STATES_AHEAD = 5
+XG_AHEAD = 3
 
 FLOPS = 2 * ROWS * HID * W_COLS
 
@@ -74,19 +76,23 @@ def tile_ircnn_lstmcell_pa_t_kernel(
         hx_sb = {}
         cx_sb = {}
 
-        def load(pair):
+        def load_states(pair):
             rows = slice(pair * PAIR, (pair + 1) * PAIR)
-            hx_pair = loads.tile([P, PAIR, HID], BF16, bufs=AHEAD + 1)
+            hx_pair = loads.tile([P, PAIR, HID], BF16, bufs=STATES_AHEAD - 1)
             nc.sync.dma_start(out=hx_pair[:], in_=hx_v[:, rows, :])
-            cx_pair = loads.tile([P, PAIR, HID], BF16, bufs=AHEAD + 3)
+            cx_pair = loads.tile([P, PAIR, HID], BF16, bufs=STATES_AHEAD + 2)
             nc.sync.dma_start(out=cx_pair[:], in_=cx_v[:, rows, :])
-            xg_pair = loads.tile([P, PAIR, GATES * HID], BF16, bufs=AHEAD + 2)
-            nc.sync.dma_start(out=xg_pair[:], in_=xg_v[:, rows, :])
             hx_sb[pair] = hx_pair
             cx_sb[pair] = cx_pair
+
+        def load_xg(pair):
+            rows = slice(pair * PAIR, (pair + 1) * PAIR)
+            xg_pair = loads.tile([P, PAIR, GATES * HID], BF16, bufs=XG_AHEAD + 2)
+            nc.sync.dma_start(out=xg_pair[:], in_=xg_v[:, rows, :])
             xg_sb[pair] = xg_pair
 
-        load(0)
+        for pair in range(BATCH // PAIR):
+            load_states(pair)
         for words, scale_rows, first, width in weights:
             for quad in range(4):
                 nc.sync.dma_start(
@@ -151,27 +157,35 @@ def tile_ircnn_lstmcell_pa_t_kernel(
             xt_bank[t] = xt
 
         def regroup(t):
-            quads = work.tile([P, 2 * P * 4], BF16, align_bytes=64, bufs=3)
+            if t % BATCH == 0:
+                quads = work.tile([P, BATCH, 2 * P * 4], BF16, align_bytes=64, bufs=2)
+                grouped[t // BATCH] = quads
             nc.scalar.copy(
-                out=quads[:].bitcast(F32).rearrange("p (w r u) -> p w r u", w=2, u=2),
+                out=grouped[t // BATCH][:, t % BATCH, :]
+                .bitcast(F32)
+                .rearrange("p (w r u) -> p w r u", w=2, u=2),
                 in_=xt_bank[t][:].rearrange("p w u r -> p w r u"),
             )
-            grouped[t] = quads
 
-        def quantise(t):
-            codes = work.tile([P, 2 * P], U32, align_bytes=64, bufs=3)
-            plane = work.tile([P, 2 * P], U8, align_bytes=64, bufs=3)
-            nc.vector.quantize_mx(out=codes[:].bitcast(FP8X4), scales=plane[:], in_=grouped[t][:])
-            x_codes[t] = codes
-            x_scales[t] = plane
+        def quantise(batch):
+            codes = work.tile([P, BATCH * 2 * P], U32, align_bytes=64, bufs=2)
+            plane = work.tile([P, BATCH * 2 * P], U8, align_bytes=64, bufs=2)
+            nc.vector.quantize_mx(
+                out=codes[:].bitcast(FP8X4),
+                scales=plane[:],
+                in_=grouped[batch][:].rearrange("p j c -> p (j c)"),
+            )
+            x_codes[batch] = codes
+            x_scales[batch] = plane
 
         def mx_pass(bank, t, which, w_first, start, stop):
-            rows = slice(which * P, (which + 1) * P)
+            first_row = ((t % BATCH) * 2 + which) * P
+            rows = slice(first_row, first_row + P)
             cols = slice(w_first, w_first + HID)
             nc.tensor.matmul_mx(
                 out=bank[:],
-                lhsT=x_codes[t][:, rows].bitcast(FP8X4),
-                lhsT_scale=x_scales[t][:, rows],
+                lhsT=x_codes[t // BATCH][:, rows].bitcast(FP8X4),
+                lhsT_scale=x_scales[t // BATCH][:, rows],
                 rhs=w_codes[:, cols].bitcast(FP8X4),
                 rhs_scale=w_scales[:, cols],
                 start=start,
@@ -241,22 +255,24 @@ def tile_ircnn_lstmcell_pa_t_kernel(
         def live(t):
             return 0 <= t < TILES
 
-        for t in range(-PAIR * (AHEAD - 1), TILES + PAIR):
-            if t % PAIR == 0 and 1 <= t // PAIR + AHEAD < PAIRS:
-                load(t // PAIR + AHEAD)
-            if live(t + 2):
-                regroup(t + 2)
+        for t in range(-6, TILES + PAIR):
+            if t % PAIR == 0 and t // PAIR + STATES_AHEAD < PAIRS:
+                load_states(t // PAIR + STATES_AHEAD)
+            if t % PAIR == 0 and t // PAIR + XG_AHEAD < PAIRS:
+                load_xg(t // PAIR + XG_AHEAD)
+            if live(t + 5):
+                regroup(t + 5)
             if live(t):
                 add_products(t)
             if live(t + 1):
                 matmuls(t + 1)
-            if live(t + 3):
-                transpose(t + 3)
+            if live(t + 6):
+                transpose(t + 6)
             if live(t):
                 activate(t)
             if live(t + 1):
                 add_bias(t + 1)
-            if live(t + 2):
-                quantise(t + 2)
+            if live(t + 5) and (t + 5) % BATCH == BATCH - 1:
+                quantise((t + 5) // BATCH)
             if t % PAIR == 0 and live(t - PAIR):
                 combine((t - PAIR) // PAIR)

@@ -24,7 +24,8 @@ WORDS = HID // 2
 W_COLS = (GATES + PEEPHOLES) * HID
 BATCH = 4
 STATES_AHEAD = 5
-XG_AHEAD = 3
+XG_AHEAD = 4
+TAIL_PAIRS = 2
 
 FLOPS = 2 * ROWS * HID * W_COLS
 
@@ -59,8 +60,8 @@ def tile_ircnn_lstmcell_pa_t_kernel(
         loads = ctx.enter_context(tc.tile_pool(name="loads", bufs=1))
         work = ctx.enter_context(tc.tile_pool(name="work", bufs=1))
         psum_bias = ctx.enter_context(tc.psum_pool(name="psum_bias", bufs=1))
-        psum_xt = ctx.enter_context(tc.psum_pool(name="psum_xt", bufs=1))
-        psum_acc = ctx.enter_context(tc.psum_pool(name="psum_acc", bufs=4))
+        psum_xt = ctx.enter_context(tc.psum_pool(name="psum_xt", bufs=2))
+        psum_acc = ctx.enter_context(tc.psum_pool(name="psum_acc", bufs=3))
         ctx.enter_context(tc.manual_schedule())
 
         w_codes = const.tile([P, W_COLS], U32, align_bytes=64)
@@ -93,6 +94,7 @@ def tile_ircnn_lstmcell_pa_t_kernel(
 
         for pair in range(BATCH // PAIR):
             load_states(pair)
+        load_xg(0)
         for words, scale_rows, first, width in weights:
             for quad in range(4):
                 nc.sync.dma_start(
@@ -203,7 +205,7 @@ def tile_ircnn_lstmcell_pa_t_kernel(
 
         def add_bias(t):
             if t % PAIR == 0:
-                gates_pair = work.tile([P, PAIR, GATES * HID], F32, bufs=4)
+                gates_pair = work.tile([P, PAIR, GATES * HID], F32, bufs=5)
                 gates_sb[t // PAIR] = gates_pair
             for gate in range(GATES):
                 cols = slice(gate * HID, (gate + 1) * HID)
@@ -224,22 +226,25 @@ def tile_ircnn_lstmcell_pa_t_kernel(
                     op=ALU.add,
                 )
 
-        def activate(t):
+        def scale_cx(t):
             if t % PAIR == 0:
                 scaled_pair = work.tile([P, PAIR, HID], F32, bufs=3)
                 cx_scaled[t // PAIR] = scaled_pair
-            mine = gates_sb[t // PAIR][:, t % PAIR, :]
             nc.scalar.activation(
                 out=cx_scaled[t // PAIR][:, t % PAIR, :],
                 in_=cx_sb[t // PAIR][:, t % PAIR, :],
                 func=ACT.Copy,
                 scale=decay[:, 0, t : t + 1],
             )
+
+        def activate(t):
+            mine = gates_sb[t // PAIR][:, t % PAIR, :]
             nc.scalar.activation(out=mine[:, 0 : 2 * HID], in_=mine[:, 0 : 2 * HID], func=ACT.Sigmoid)
             nc.scalar.activation(out=mine[:, 2 * HID :], in_=mine[:, 2 * HID :], func=ACT.Tanh)
-            nc.scalar.activation(
-                out=mine[:, 2 * HID :], in_=mine[:, 2 * HID :], func=ACT.Copy, scale=decay[:, 1, t : t + 1]
-            )
+
+        def scale_g(t):
+            g_g = gates_sb[t // PAIR][:, t % PAIR, 2 * HID :]
+            nc.scalar.activation(out=g_g, in_=g_g, func=ACT.Copy, scale=decay[:, 1, t : t + 1])
 
         def combine(pair):
             acts = gates_sb[pair]
@@ -252,13 +257,42 @@ def tile_ircnn_lstmcell_pa_t_kernel(
             nc.gpsimd.tensor_tensor(out=new_c[:], in0=i_g, in1=f_g, op=ALU.add)
             nc.sync.dma_start(out=out_v[:, pair * PAIR : (pair + 1) * PAIR, :], in_=new_c[:])
 
+        tail_c = {}
+
+        def combine_on_vector(t):
+            if t % PAIR == 0:
+                tail_pair = work.tile([P, PAIR, HID], F32, bufs=2)
+                tail_c[t // PAIR] = tail_pair
+            mine = gates_sb[t // PAIR][:, t % PAIR, :]
+            i_g = mine[:, 0:HID]
+            f_g = mine[:, HID : 2 * HID]
+            g_g = mine[:, 2 * HID :]
+            nc.vector.scalar_tensor_tensor(
+                out=f_g,
+                in0=f_g,
+                scalar=decay[:, 0, t : t + 1],
+                in1=cx_sb[t // PAIR][:, t % PAIR, :],
+                op0=ALU.mult,
+                op1=ALU.mult,
+            )
+            nc.vector.scalar_tensor_tensor(
+                out=i_g, in0=i_g, scalar=decay[:, 1, t : t + 1], in1=g_g, op0=ALU.mult, op1=ALU.mult
+            )
+            nc.vector.tensor_tensor(out=tail_c[t // PAIR][:, t % PAIR, :], in0=i_g, in1=f_g, op=ALU.add)
+            if t % PAIR == PAIR - 1:
+                rows = slice(t + 1 - PAIR, t + 1)
+                nc.sync.dma_start(out=out_v[:, rows, :], in_=tail_c[t // PAIR][:])
+
         def live(t):
             return 0 <= t < TILES
+
+        def in_tail(t):
+            return t // PAIR >= PAIRS - TAIL_PAIRS
 
         for t in range(-6, TILES + PAIR):
             if t % PAIR == 0 and t // PAIR + STATES_AHEAD < PAIRS:
                 load_states(t // PAIR + STATES_AHEAD)
-            if t % PAIR == 0 and t // PAIR + XG_AHEAD < PAIRS:
+            if t % PAIR == 0 and 1 <= t // PAIR + XG_AHEAD < PAIRS:
                 load_xg(t // PAIR + XG_AHEAD)
             if live(t + 5):
                 regroup(t + 5)
@@ -268,11 +302,17 @@ def tile_ircnn_lstmcell_pa_t_kernel(
                 matmuls(t + 1)
             if live(t + 6):
                 transpose(t + 6)
+            if live(t) and not in_tail(t):
+                scale_cx(t)
             if live(t):
                 activate(t)
-            if live(t + 1):
-                add_bias(t + 1)
+            if live(t) and not in_tail(t):
+                scale_g(t)
+            if live(t - 1) and in_tail(t - 1):
+                combine_on_vector(t - 1)
+            if live(t + 3):
+                add_bias(t + 3)
             if live(t + 5) and (t + 5) % BATCH == BATCH - 1:
                 quantise((t + 5) // BATCH)
-            if t % PAIR == 0 and live(t - PAIR):
+            if t % PAIR == 0 and live(t - PAIR) and not in_tail(t - PAIR):
                 combine((t - PAIR) // PAIR)

@@ -64,6 +64,41 @@ def tile_ircnn_lstmcell_pa_t_kernel(
         psum_acc = ctx.enter_context(tc.psum_pool(name="psum_acc", bufs=3))
         ctx.enter_context(tc.manual_schedule())
 
+        bias_row = const.tile([P, GATES * HID], BF16)
+        nc.vector.memset(bias_row[:], 0.0)
+        nc.sync.dma_start(out=bias_row[0:1, :], in_=b_hh.rearrange("(o c) -> o c", o=1))
+        ones = const.tile([P, P], BF16)
+        nc.vector.memset(ones[:], 1.0)
+        bias_bank = []
+        for gate in range(GATES):
+            bank = psum_bias.tile([P, HID], F32, name="bias_bank%d" % gate)
+            nc.tensor.matmul(
+                out=bank[:],
+                lhsT=ones[:],
+                rhs=bias_row[:, gate * HID : (gate + 1) * HID],
+                start=True,
+                stop=True,
+            )
+            bias_bank.append(bank)
+
+        ident = const.tile([P, P], F32)
+        make_identity(nc, ident[:])
+
+        a_bf = const.tile([P, 1], BF16)
+        nc.scalar.dma_start(out=a_bf[:], in_=a.partition_broadcast(P))
+        b_bf = const.tile([P, 1], BF16)
+        nc.scalar.dma_start(out=b_bf[:], in_=b.partition_broadcast(P))
+        td_sb = const.tile([P, 2, TILES], BF16)
+        nc.scalar.dma_start(out=td_sb[:, 0, :], in_=td0.rearrange("(p t) -> p t", t=TILES))
+        nc.scalar.dma_start(out=td_sb[:, 1, :], in_=td1.rearrange("(p t) -> p t", t=TILES))
+        a_f32 = const.tile([P, 1], F32)
+        nc.scalar.copy(out=a_f32[:], in_=a_bf[:])
+        minus_b = const.tile([P, 1], F32)
+        nc.scalar.mul(out=minus_b[:], in_=b_bf[:], mul=-1.0)
+        decay = const.tile([P, 2, TILES], F32)
+        nc.scalar.activation(out=decay[:], in_=td_sb[:], func=ACT.Exp, scale=minus_b[:, 0:1])
+        nc.scalar.activation(out=decay[:], in_=decay[:], func=ACT.Copy, scale=a_f32[:, 0:1])
+
         w_codes = const.tile([P, W_COLS], U32, align_bytes=64)
         w_scales = const.tile([P, W_COLS], U8, align_bytes=64)
         nc.vector.memset(w_scales[:].bitcast(I32), 0)
@@ -92,9 +127,9 @@ def tile_ircnn_lstmcell_pa_t_kernel(
             nc.sync.dma_start(out=xg_pair[:], in_=xg_v[:, rows, :])
             xg_sb[pair] = xg_pair
 
+        load_xg(0)
         for pair in range(BATCH // PAIR):
             load_states(pair)
-        load_xg(0)
         for words, scale_rows, first, width in weights:
             for quad in range(4):
                 nc.sync.dma_start(
@@ -106,41 +141,6 @@ def tile_ircnn_lstmcell_pa_t_kernel(
                 out=w_codes[:, first : first + width].bitcast(I32),
                 in_=words[0].rearrange("p n t -> p (n t)").bitcast(I32),
             )
-
-        ident = const.tile([P, P], F32)
-        make_identity(nc, ident[:])
-
-        bias_row = const.tile([P, GATES * HID], BF16)
-        nc.vector.memset(bias_row[:], 0.0)
-        nc.scalar.dma_start(out=bias_row[0:1, :], in_=b_hh.rearrange("(o c) -> o c", o=1))
-        ones = const.tile([P, P], BF16)
-        nc.vector.memset(ones[:], 1.0)
-        bias_bank = []
-        for gate in range(GATES):
-            bank = psum_bias.tile([P, HID], F32, name="bias_bank%d" % gate)
-            nc.tensor.matmul(
-                out=bank[:],
-                lhsT=ones[:],
-                rhs=bias_row[:, gate * HID : (gate + 1) * HID],
-                start=True,
-                stop=True,
-            )
-            bias_bank.append(bank)
-
-        a_bf = const.tile([P, 1], BF16)
-        nc.scalar.dma_start(out=a_bf[:], in_=a.partition_broadcast(P))
-        b_bf = const.tile([P, 1], BF16)
-        nc.scalar.dma_start(out=b_bf[:], in_=b.partition_broadcast(P))
-        td_sb = const.tile([P, 2, TILES], BF16)
-        nc.scalar.dma_start(out=td_sb[:, 0, :], in_=td0.rearrange("(p t) -> p t", t=TILES))
-        nc.scalar.dma_start(out=td_sb[:, 1, :], in_=td1.rearrange("(p t) -> p t", t=TILES))
-        a_f32 = const.tile([P, 1], F32)
-        nc.vector.tensor_copy(out=a_f32[:], in_=a_bf[:])
-        minus_b = const.tile([P, 1], F32)
-        nc.vector.tensor_scalar_mul(out=minus_b[:], in0=b_bf[:], scalar1=-1.0)
-        decay = const.tile([P, 2, TILES], F32)
-        nc.scalar.activation(out=decay[:], in_=td_sb[:], func=ACT.Exp, scale=minus_b[:, 0:1])
-        nc.vector.tensor_scalar_mul(out=decay[:], in0=decay[:], scalar1=a_f32[:, 0:1])
 
         xt_bank = {}
         grouped = {}
@@ -289,7 +289,7 @@ def tile_ircnn_lstmcell_pa_t_kernel(
         def in_tail(t):
             return t // PAIR >= PAIRS - TAIL_PAIRS
 
-        for t in range(-6, TILES + PAIR):
+        for t in range(-6, TILES):
             if t % PAIR == 0 and t // PAIR + STATES_AHEAD < PAIRS:
                 load_states(t // PAIR + STATES_AHEAD)
             if t % PAIR == 0 and 1 <= t // PAIR + XG_AHEAD < PAIRS:
@@ -308,11 +308,11 @@ def tile_ircnn_lstmcell_pa_t_kernel(
                 activate(t)
             if live(t) and not in_tail(t):
                 scale_g(t)
-            if live(t - 1) and in_tail(t - 1):
-                combine_on_vector(t - 1)
             if live(t + 3):
                 add_bias(t + 3)
             if live(t + 5) and (t + 5) % BATCH == BATCH - 1:
                 quantise((t + 5) // BATCH)
             if t % PAIR == 0 and live(t - PAIR) and not in_tail(t - PAIR):
                 combine((t - PAIR) // PAIR)
+        for t in range(TILES - TAIL_PAIRS * PAIR, TILES):
+            combine_on_vector(t)

@@ -64,6 +64,15 @@ def tile_ircnn_lstmcell_pa_t_kernel(
         psum_acc = ctx.enter_context(tc.psum_pool(name="psum_acc", bufs=3))
         ctx.enter_context(tc.manual_schedule())
 
+        w_codes = const.tile([P, W_COLS], U32, align_bytes=64)
+        w_scales = const.tile([P, W_COLS], U8, align_bytes=64)
+        nc.vector.memset(w_scales[:].bitcast(I32), 0)
+        weights = (
+            (w_hh_words, w_hh_scales, 0, GATES * HID),
+            (w_pi_words, w_pi_scales, GATES * HID, HID),
+            (w_pf_words, w_pf_scales, GATES * HID + HID, HID),
+        )
+
         bias_row = const.tile([P, GATES * HID], BF16)
         nc.vector.memset(bias_row[:], 0.0)
         nc.sync.dma_start(out=bias_row[0:1, :], in_=b_hh.rearrange("(o c) -> o c", o=1))
@@ -84,30 +93,6 @@ def tile_ircnn_lstmcell_pa_t_kernel(
         ident = const.tile([P, P], F32)
         make_identity(nc, ident[:])
 
-        a_bf = const.tile([P, 1], BF16)
-        nc.scalar.dma_start(out=a_bf[:], in_=a.partition_broadcast(P))
-        b_bf = const.tile([P, 1], BF16)
-        nc.scalar.dma_start(out=b_bf[:], in_=b.partition_broadcast(P))
-        td_sb = const.tile([P, 2, TILES], BF16)
-        nc.scalar.dma_start(out=td_sb[:, 0, :], in_=td0.rearrange("(p t) -> p t", t=TILES))
-        nc.scalar.dma_start(out=td_sb[:, 1, :], in_=td1.rearrange("(p t) -> p t", t=TILES))
-        a_f32 = const.tile([P, 1], F32)
-        nc.scalar.copy(out=a_f32[:], in_=a_bf[:])
-        minus_b = const.tile([P, 1], F32)
-        nc.scalar.mul(out=minus_b[:], in_=b_bf[:], mul=-1.0)
-        decay = const.tile([P, 2, TILES], F32)
-        nc.scalar.activation(out=decay[:], in_=td_sb[:], func=ACT.Exp, scale=minus_b[:, 0:1])
-        nc.scalar.activation(out=decay[:], in_=decay[:], func=ACT.Copy, scale=a_f32[:, 0:1])
-
-        w_codes = const.tile([P, W_COLS], U32, align_bytes=64)
-        w_scales = const.tile([P, W_COLS], U8, align_bytes=64)
-        nc.vector.memset(w_scales[:].bitcast(I32), 0)
-        weights = (
-            (w_hh_words, w_hh_scales, 0, GATES * HID),
-            (w_pi_words, w_pi_scales, GATES * HID, HID),
-            (w_pf_words, w_pf_scales, GATES * HID + HID, HID),
-        )
-
         xg_sb = {}
         hx_sb = {}
         cx_sb = {}
@@ -127,20 +112,56 @@ def tile_ircnn_lstmcell_pa_t_kernel(
             nc.sync.dma_start(out=xg_pair[:], in_=xg_v[:, rows, :])
             xg_sb[pair] = xg_pair
 
-        load_xg(0)
-        for pair in range(BATCH // PAIR):
-            load_states(pair)
-        for words, scale_rows, first, width in weights:
+        def load_scales(which):
+            words, scale_rows, first, width = weights[which]
             for quad in range(4):
                 nc.sync.dma_start(
                     out=w_scales[32 * quad : 32 * quad + 4, first : first + width].bitcast(I32),
                     in_=scale_rows[0, 4 * quad : 4 * quad + 4, :].bitcast(I32),
                 )
-        for words, scale_rows, first, width in weights:
+
+        def load_codes(which):
+            words, scale_rows, first, width = weights[which]
             nc.sync.dma_start(
                 out=w_codes[:, first : first + width].bitcast(I32),
                 in_=words[0].rearrange("p n t -> p (n t)").bitcast(I32),
             )
+
+        a_bf = const.tile([P, 1], BF16)
+        b_bf = const.tile([P, 1], BF16)
+        td_sb = const.tile([P, 2, TILES], BF16)
+        decay = const.tile([P, 2, TILES], F32)
+
+        def load_decay_inputs():
+            nc.sync.dma_start(out=a_bf[:], in_=a.partition_broadcast(P))
+            nc.sync.dma_start(out=b_bf[:], in_=b.partition_broadcast(P))
+            nc.sync.dma_start(out=td_sb[:, 0, :], in_=td0.rearrange("(p t) -> p t", t=TILES))
+            nc.sync.dma_start(out=td_sb[:, 1, :], in_=td1.rearrange("(p t) -> p t", t=TILES))
+
+        def make_decay():
+            a_f32 = const.tile([P, 1], F32)
+            nc.scalar.copy(out=a_f32[:], in_=a_bf[:])
+            minus_b = const.tile([P, 1], F32)
+            nc.scalar.mul(out=minus_b[:], in_=b_bf[:], mul=-1.0)
+            nc.scalar.activation(out=decay[:], in_=td_sb[:], func=ACT.Exp, scale=minus_b[:, 0:1])
+            nc.scalar.activation(out=decay[:], in_=decay[:], func=ACT.Copy, scale=a_f32[:, 0:1])
+            warm = const.tile([P, 1], F32)
+            nc.scalar.activation(out=warm[:], in_=a_f32[:], func=ACT.Sigmoid)
+
+        load_scales(0)
+        load_states(0)
+        load_codes(0)
+        load_codes(1)
+        load_scales(1)
+        load_xg(0)
+        load_decay_inputs()
+        load_codes(2)
+        load_scales(2)
+        load_states(1)
+        load_xg(1)
+        load_states(2)
+        load_states(3)
+        load_xg(2)
 
         xt_bank = {}
         grouped = {}
@@ -169,16 +190,18 @@ def tile_ircnn_lstmcell_pa_t_kernel(
                 in_=xt_bank[t][:].rearrange("p w u r -> p w r u"),
             )
 
-        def quantise(batch):
-            codes = work.tile([P, BATCH * 2 * P], U32, align_bytes=64, bufs=2)
-            plane = work.tile([P, BATCH * 2 * P], U8, align_bytes=64, bufs=2)
+        def quantise(batch, first_tile=0, tiles=BATCH):
+            if first_tile == 0:
+                codes = work.tile([P, BATCH * 2 * P], U32, align_bytes=64, bufs=2)
+                plane = work.tile([P, BATCH * 2 * P], U8, align_bytes=64, bufs=2)
+                x_codes[batch] = codes
+                x_scales[batch] = plane
+            cols = slice(first_tile * 2 * P, (first_tile + tiles) * 2 * P)
             nc.vector.quantize_mx(
-                out=codes[:].bitcast(FP8X4),
-                scales=plane[:],
-                in_=grouped[batch][:].rearrange("p j c -> p (j c)"),
+                out=x_codes[batch][:, cols].bitcast(FP8X4),
+                scales=x_scales[batch][:, cols],
+                in_=grouped[batch][:, first_tile : first_tile + tiles, :].rearrange("p j c -> p (j c)"),
             )
-            x_codes[batch] = codes
-            x_scales[batch] = plane
 
         def mx_pass(bank, t, which, w_first, start, stop):
             first_row = ((t % BATCH) * 2 + which) * P
@@ -289,28 +312,48 @@ def tile_ircnn_lstmcell_pa_t_kernel(
         def in_tail(t):
             return t // PAIR >= PAIRS - TAIL_PAIRS
 
-        for t in range(-6, TILES):
+        def to_transpose(t):
+            return (2 * t + 4, 2 * t + 5) if t < 2 else (t + 6,)
+
+        def to_regroup(t):
+            return (2 * t + 2, 2 * t + 3) if t < 3 else (t + 5,)
+
+        for t in range(-2, TILES):
             if t % PAIR == 0 and t // PAIR + STATES_AHEAD < PAIRS:
                 load_states(t // PAIR + STATES_AHEAD)
-            if t % PAIR == 0 and 1 <= t // PAIR + XG_AHEAD < PAIRS:
+            if t % PAIR == 0 and t // PAIR + XG_AHEAD < PAIRS:
                 load_xg(t // PAIR + XG_AHEAD)
-            if live(t + 5):
-                regroup(t + 5)
+            for x in to_regroup(t):
+                if live(x):
+                    regroup(x)
+            if t == -1:
+                make_decay()
+                quantise(0, 0, PAIR)
+                add_bias(0)
+                add_bias(1)
             if live(t):
                 add_products(t)
             if live(t + 1):
                 matmuls(t + 1)
-            if live(t + 6):
-                transpose(t + 6)
+            for x in to_transpose(t):
+                if live(x):
+                    transpose(x)
             if live(t) and not in_tail(t):
                 scale_cx(t)
             if live(t):
                 activate(t)
             if live(t) and not in_tail(t):
                 scale_g(t)
-            if live(t + 3):
+            if t == 0:
+                add_bias(2)
+                quantise(0, PAIR, PAIR)
+            if t == 1:
+                add_bias(3)
+            if t == 2:
+                add_bias(4)
+            if t >= 2 and live(t + 3):
                 add_bias(t + 3)
-            if live(t + 5) and (t + 5) % BATCH == BATCH - 1:
+            if t >= 2 and live(t + 5) and (t + 5) % BATCH == BATCH - 1:
                 quantise((t + 5) // BATCH)
             if t % PAIR == 0 and live(t - PAIR) and not in_tail(t - PAIR):
                 combine((t - PAIR) // PAIR)

@@ -25,6 +25,7 @@ W_COLS = (GATES + PEEPHOLES) * HID
 BATCH = 4
 STATES_AHEAD = 5
 XG_AHEAD = 4
+PE_EVERY = 3
 TAIL_PAIRS = 2
 
 FLOPS = 2 * ROWS * HID * W_COLS
@@ -61,6 +62,7 @@ def tile_ircnn_lstmcell_pa_t_kernel(
         work = ctx.enter_context(tc.tile_pool(name="work", bufs=1))
         psum_bias = ctx.enter_context(tc.psum_pool(name="psum_bias", bufs=1))
         psum_xt = ctx.enter_context(tc.psum_pool(name="psum_xt", bufs=2))
+        psum_xgb = ctx.enter_context(tc.psum_pool(name="psum_xgb", bufs=1))
         psum_acc = ctx.enter_context(tc.psum_pool(name="psum_acc", bufs=3))
         ctx.enter_context(tc.manual_schedule())
 
@@ -78,17 +80,19 @@ def tile_ircnn_lstmcell_pa_t_kernel(
         nc.sync.dma_start(out=bias_row[0:1, :], in_=b_hh.rearrange("(o c) -> o c", o=1))
         ones = const.tile([P, P], BF16)
         nc.vector.memset(ones[:], 1.0)
-        bias_bank = []
+        bias_if = psum_bias.tile([P, PEEPHOLES * HID], BF16, name="bias_if")
+        bias_g = psum_bias.tile([P, HID], BF16, name="bias_g")
+        bias_bank = [bias_if[:, 0:HID], bias_if[:, HID : 2 * HID], bias_g[:]]
         for gate in range(GATES):
-            bank = psum_bias.tile([P, HID], F32, name="bias_bank%d" % gate)
             nc.tensor.matmul(
-                out=bank[:],
+                out=bias_bank[gate],
                 lhsT=ones[:],
                 rhs=bias_row[:, gate * HID : (gate + 1) * HID],
                 start=True,
                 stop=True,
             )
-            bias_bank.append(bank)
+        ident_bf = const.tile([P, P], BF16)
+        make_identity(nc, ident_bf[:])
 
         ident = const.tile([P, P], F32)
         make_identity(nc, ident[:])
@@ -226,16 +230,38 @@ def tile_ircnn_lstmcell_pa_t_kernel(
                     mx_pass(bank, t, 1, (GATES + gate) * HID, False, True)
                 acc[(t, gate)] = bank
 
+        def by_pe(t, gate):
+            return gate == GATES - 1 and t >= PAIR and t % PE_EVERY == 0
+
+        xgb_bank = {}
+
+        def pe_bias(t):
+            for gate in range(GATES):
+                if by_pe(t, gate):
+                    cols = slice(gate * HID, (gate + 1) * HID)
+                    bank = psum_xgb.tile([P, HID], F32)
+                    nc.tensor.matmul(out=bank[:], lhsT=ident_bf[:], rhs=xg_sb[t // PAIR][:, t % PAIR, cols], start=True, stop=False)
+                    nc.tensor.matmul(out=bank[:], lhsT=ones[:], rhs=bias_row[:, cols], start=False, stop=True)
+                    xgb_bank[(t, gate)] = bank
+
+        def copy_bias(t):
+            for gate in range(GATES):
+                if by_pe(t, gate):
+                    cols = slice(gate * HID, (gate + 1) * HID)
+                    nc.scalar.copy(out=gates_sb[t // PAIR][:, t % PAIR, cols], in_=xgb_bank[(t, gate)][:])
+
         def add_bias(t):
             if t % PAIR == 0:
                 gates_pair = work.tile([P, PAIR, GATES * HID], F32, bufs=5)
                 gates_sb[t // PAIR] = gates_pair
             for gate in range(GATES):
+                if by_pe(t, gate):
+                    continue
                 cols = slice(gate * HID, (gate + 1) * HID)
                 nc.vector.tensor_tensor(
                     out=gates_sb[t // PAIR][:, t % PAIR, cols],
                     in0=xg_sb[t // PAIR][:, t % PAIR, cols],
-                    in1=bias_bank[gate][:],
+                    in1=bias_bank[gate],
                     op=ALU.add,
                 )
 
@@ -330,7 +356,11 @@ def tile_ircnn_lstmcell_pa_t_kernel(
                 make_decay()
                 quantise(0, 0, PAIR)
                 add_bias(0)
+                pe_bias(0)
+                copy_bias(0)
                 add_bias(1)
+                pe_bias(1)
+                copy_bias(1)
             if live(t):
                 add_products(t)
             if live(t + 1):
@@ -346,13 +376,21 @@ def tile_ircnn_lstmcell_pa_t_kernel(
                 scale_g(t)
             if t == 0:
                 add_bias(2)
+                pe_bias(2)
+                copy_bias(2)
                 quantise(0, PAIR, PAIR)
             if t == 1:
                 add_bias(3)
+                pe_bias(3)
+                copy_bias(3)
             if t == 2:
                 add_bias(4)
+                pe_bias(4)
+                copy_bias(4)
             if t >= 2 and live(t + 3):
                 add_bias(t + 3)
+                pe_bias(t + 3)
+                copy_bias(t + 3)
             if t >= 2 and live(t + 5) and (t + 5) % BATCH == BATCH - 1:
                 quantise((t + 5) // BATCH)
             if t % PAIR == 0 and live(t - PAIR) and not in_tail(t - PAIR):

@@ -25,7 +25,8 @@ W_COLS = (GATES + PEEPHOLES) * HID
 BATCH = 4
 STATES_AHEAD = 5
 XG_AHEAD = 4
-PE_EVERY = 3
+F_AHEAD = 3
+GATE_BUFS = 6
 TAIL_PAIRS = 2
 
 FLOPS = 2 * ROWS * HID * W_COLS
@@ -63,6 +64,7 @@ def tile_ircnn_lstmcell_pa_t_kernel(
         psum_bias = ctx.enter_context(tc.psum_pool(name="psum_bias", bufs=1))
         psum_xt = ctx.enter_context(tc.psum_pool(name="psum_xt", bufs=2))
         psum_xgb = ctx.enter_context(tc.psum_pool(name="psum_xgb", bufs=1))
+        psum_cx = ctx.enter_context(tc.psum_pool(name="psum_cx", bufs=1))
         psum_acc = ctx.enter_context(tc.psum_pool(name="psum_acc", bufs=3))
         ctx.enter_context(tc.manual_schedule())
 
@@ -80,10 +82,9 @@ def tile_ircnn_lstmcell_pa_t_kernel(
         nc.sync.dma_start(out=bias_row[0:1, :], in_=b_hh.rearrange("(o c) -> o c", o=1))
         ones = const.tile([P, P], BF16)
         nc.vector.memset(ones[:], 1.0)
-        bias_if = psum_bias.tile([P, PEEPHOLES * HID], BF16, name="bias_if")
-        bias_g = psum_bias.tile([P, HID], BF16, name="bias_g")
-        bias_bank = [bias_if[:, 0:HID], bias_if[:, HID : 2 * HID], bias_g[:]]
-        for gate in range(GATES):
+        bias_ig = psum_bias.tile([P, 2 * HID], BF16, name="bias_ig")
+        bias_bank = [bias_ig[:, 0:HID], None, bias_ig[:, HID : 2 * HID]]
+        for gate in (0, 2):
             nc.tensor.matmul(
                 out=bias_bank[gate],
                 lhsT=ones[:],
@@ -91,6 +92,10 @@ def tile_ircnn_lstmcell_pa_t_kernel(
                 start=True,
                 stop=True,
             )
+        bias_f_ps = psum_xgb.tile([P, HID], F32, name="xgb")
+        nc.tensor.matmul(out=bias_f_ps[:], lhsT=ones[:], rhs=bias_row[:, HID : 2 * HID], start=True, stop=True)
+        bias_f = const.tile([P, HID], F32)
+        nc.scalar.copy(out=bias_f[:], in_=bias_f_ps[:])
         ident_bf = const.tile([P, P], BF16)
         make_identity(nc, ident_bf[:])
 
@@ -173,7 +178,6 @@ def tile_ircnn_lstmcell_pa_t_kernel(
         x_scales = {}
         acc = {}
         gates_sb = {}
-        cx_scaled = {}
 
         def transpose(t):
             xt = psum_xt.tile([P, 2, 2, P], F32)
@@ -231,7 +235,7 @@ def tile_ircnn_lstmcell_pa_t_kernel(
                 acc[(t, gate)] = bank
 
         def by_pe(t, gate):
-            return gate == GATES - 1 and t >= PAIR and t % PE_EVERY == 0
+            return gate == GATES - 1 and t >= 2 * PAIR and t % PAIR == 0
 
         xgb_bank = {}
 
@@ -239,7 +243,7 @@ def tile_ircnn_lstmcell_pa_t_kernel(
             for gate in range(GATES):
                 if by_pe(t, gate):
                     cols = slice(gate * HID, (gate + 1) * HID)
-                    bank = psum_xgb.tile([P, HID], F32)
+                    bank = psum_xgb.tile([P, HID], F32, name="xgb")
                     nc.tensor.matmul(out=bank[:], lhsT=ident_bf[:], rhs=xg_sb[t // PAIR][:, t % PAIR, cols], start=True, stop=False)
                     nc.tensor.matmul(out=bank[:], lhsT=ones[:], rhs=bias_row[:, cols], start=False, stop=True)
                     xgb_bank[(t, gate)] = bank
@@ -250,12 +254,32 @@ def tile_ircnn_lstmcell_pa_t_kernel(
                     cols = slice(gate * HID, (gate + 1) * HID)
                     nc.scalar.copy(out=gates_sb[t // PAIR][:, t % PAIR, cols], in_=xgb_bank[(t, gate)][:])
 
+        def add_bias_f(pair):
+            gates_pair = work.tile([P, PAIR, GATES * HID], F32, bufs=GATE_BUFS)
+            gates_sb[pair] = gates_pair
+            nc.gpsimd.tensor_tensor(
+                out=gates_pair[:, :, HID : 2 * HID],
+                in0=xg_sb[pair][:, :, HID : 2 * HID],
+                in1=bias_f[:].unsqueeze(1).to_broadcast([P, PAIR, HID]),
+                op=ALU.add,
+            )
+
+        cx_bank = {}
+
+        def cx_to_psum(t):
+            bank = psum_cx.tile([P, HID], F32)
+            nc.tensor.matmul(out=bank[:], lhsT=ident_bf[:], rhs=cx_sb[t // PAIR][:, t % PAIR, :], start=True, stop=True)
+            cx_bank[t] = bank
+
+        def forget_term(t):
+            f_g = gates_sb[t // PAIR][:, t % PAIR, HID : 2 * HID]
+            nc.vector.scalar_tensor_tensor(
+                out=f_g, in0=cx_bank[t][:], scalar=decay[:, 0, t : t + 1], in1=f_g, op0=ALU.mult, op1=ALU.mult
+            )
+
         def add_bias(t):
-            if t % PAIR == 0:
-                gates_pair = work.tile([P, PAIR, GATES * HID], F32, bufs=5)
-                gates_sb[t // PAIR] = gates_pair
             for gate in range(GATES):
-                if by_pe(t, gate):
+                if by_pe(t, gate) or gate == 1:
                     continue
                 cols = slice(gate * HID, (gate + 1) * HID)
                 nc.vector.tensor_tensor(
@@ -275,17 +299,6 @@ def tile_ircnn_lstmcell_pa_t_kernel(
                     op=ALU.add,
                 )
 
-        def scale_cx(t):
-            if t % PAIR == 0:
-                scaled_pair = work.tile([P, PAIR, HID], F32, bufs=3)
-                cx_scaled[t // PAIR] = scaled_pair
-            nc.scalar.activation(
-                out=cx_scaled[t // PAIR][:, t % PAIR, :],
-                in_=cx_sb[t // PAIR][:, t % PAIR, :],
-                func=ACT.Copy,
-                scale=decay[:, 0, t : t + 1],
-            )
-
         def activate(t):
             mine = gates_sb[t // PAIR][:, t % PAIR, :]
             nc.scalar.activation(out=mine[:, 0 : 2 * HID], in_=mine[:, 0 : 2 * HID], func=ACT.Sigmoid)
@@ -301,7 +314,6 @@ def tile_ircnn_lstmcell_pa_t_kernel(
             f_g = acts[:, :, HID : 2 * HID]
             g_g = acts[:, :, 2 * HID :]
             new_c = work.tile([P, PAIR, HID], F32, bufs=3)
-            nc.gpsimd.tensor_tensor(out=f_g, in0=f_g, in1=cx_scaled[pair][:], op=ALU.mult)
             nc.gpsimd.tensor_tensor(out=i_g, in0=i_g, in1=g_g, op=ALU.mult)
             nc.gpsimd.tensor_tensor(out=new_c[:], in0=i_g, in1=f_g, op=ALU.add)
             nc.sync.dma_start(out=out_v[:, pair * PAIR : (pair + 1) * PAIR, :], in_=new_c[:])
@@ -317,14 +329,6 @@ def tile_ircnn_lstmcell_pa_t_kernel(
             f_g = mine[:, HID : 2 * HID]
             g_g = mine[:, 2 * HID :]
             nc.vector.scalar_tensor_tensor(
-                out=f_g,
-                in0=f_g,
-                scalar=decay[:, 0, t : t + 1],
-                in1=cx_sb[t // PAIR][:, t % PAIR, :],
-                op0=ALU.mult,
-                op1=ALU.mult,
-            )
-            nc.vector.scalar_tensor_tensor(
                 out=i_g, in0=i_g, scalar=decay[:, 1, t : t + 1], in1=g_g, op0=ALU.mult, op1=ALU.mult
             )
             nc.vector.tensor_tensor(out=tail_c[t // PAIR][:, t % PAIR, :], in0=i_g, in1=f_g, op=ALU.add)
@@ -339,10 +343,10 @@ def tile_ircnn_lstmcell_pa_t_kernel(
             return t // PAIR >= PAIRS - TAIL_PAIRS
 
         def to_transpose(t):
-            return (2 * t + 4, 2 * t + 5) if t < 2 else (t + 6,)
+            return (2 * t + 4, 2 * t + 5) if t < 3 else (t + 7,)
 
         def to_regroup(t):
-            return (2 * t + 2, 2 * t + 3) if t < 3 else (t + 5,)
+            return (2 * t + 2, 2 * t + 3) if t < 4 else (t + 6,)
 
         for t in range(-2, TILES):
             if t % PAIR == 0 and t // PAIR + STATES_AHEAD < PAIRS:
@@ -353,6 +357,8 @@ def tile_ircnn_lstmcell_pa_t_kernel(
                 if live(x):
                     regroup(x)
             if t == -1:
+                for pair in range(F_AHEAD):
+                    add_bias_f(pair)
                 make_decay()
                 quantise(0, 0, PAIR)
                 add_bias(0)
@@ -361,15 +367,19 @@ def tile_ircnn_lstmcell_pa_t_kernel(
                 add_bias(1)
                 pe_bias(1)
                 copy_bias(1)
+            if t % PAIR == 0 and t >= 0 and t // PAIR + F_AHEAD < PAIRS:
+                add_bias_f(t // PAIR + F_AHEAD)
             if live(t):
                 add_products(t)
             if live(t + 1):
                 matmuls(t + 1)
+            if live(t - 1):
+                forget_term(t - 1)
+            if live(t):
+                cx_to_psum(t)
             for x in to_transpose(t):
                 if live(x):
                     transpose(x)
-            if live(t) and not in_tail(t):
-                scale_cx(t)
             if live(t):
                 activate(t)
             if live(t) and not in_tail(t):
@@ -395,5 +405,6 @@ def tile_ircnn_lstmcell_pa_t_kernel(
                 quantise((t + 5) // BATCH)
             if t % PAIR == 0 and live(t - PAIR) and not in_tail(t - PAIR):
                 combine((t - PAIR) // PAIR)
+        forget_term(TILES - 1)
         for t in range(TILES - TAIL_PAIRS * PAIR, TILES):
             combine_on_vector(t)

@@ -367,16 +367,11 @@ def tile_ircnn_lstmcell_pa_t_kernel(
                 add_bias(1)
                 pe_bias(1)
                 copy_bias(1)
-            if t % PAIR == 0 and t >= 0 and t // PAIR + F_AHEAD < PAIRS:
-                add_bias_f(t // PAIR + F_AHEAD)
             if live(t):
                 add_products(t)
             if live(t + 1):
                 matmuls(t + 1)
-            if live(t - 1):
-                forget_term(t - 1)
-            if live(t):
-                cx_to_psum(t)
+
             for x in to_transpose(t):
                 if live(x):
                     transpose(x)
@@ -403,8 +398,14 @@ def tile_ircnn_lstmcell_pa_t_kernel(
                 copy_bias(t + 3)
             if t >= 2 and live(t + 5) and (t + 5) % BATCH == BATCH - 1:
                 quantise((t + 5) // BATCH)
+            if live(t - 1):
+                forget_term(t - 1)
+            if live(t):
+                cx_to_psum(t)
             if t % PAIR == 0 and live(t - PAIR) and not in_tail(t - PAIR):
                 combine((t - PAIR) // PAIR)
+            if t % PAIR == 0 and t >= 0 and t // PAIR + F_AHEAD < PAIRS:
+                add_bias_f(t // PAIR + F_AHEAD)
         forget_term(TILES - 1)
         for t in range(TILES - TAIL_PAIRS * PAIR, TILES):
             combine_on_vector(t)

@@ -82,20 +82,21 @@ def tile_ircnn_lstmcell_pa_t_kernel(
         nc.sync.dma_start(out=bias_row[0:1, :], in_=b_hh.rearrange("(o c) -> o c", o=1))
         ones = const.tile([P, P], BF16)
         nc.vector.memset(ones[:], 1.0)
-        bias_ig = psum_bias.tile([P, 2 * HID], BF16, name="bias_ig")
-        bias_bank = [bias_ig[:, 0:HID], None, bias_ig[:, HID : 2 * HID]]
-        for gate in (0, 2):
+        bias_if = psum_bias.tile([P, PEEPHOLES * HID], BF16, name="bias_if")
+        for gate in range(PEEPHOLES):
             nc.tensor.matmul(
-                out=bias_bank[gate],
+                out=bias_if[:, gate * HID : (gate + 1) * HID],
                 lhsT=ones[:],
                 rhs=bias_row[:, gate * HID : (gate + 1) * HID],
                 start=True,
                 stop=True,
             )
-        bias_f_ps = psum_xgb.tile([P, HID], F32, name="xgb")
-        nc.tensor.matmul(out=bias_f_ps[:], lhsT=ones[:], rhs=bias_row[:, HID : 2 * HID], start=True, stop=True)
-        bias_f = const.tile([P, HID], F32)
-        nc.scalar.copy(out=bias_f[:], in_=bias_f_ps[:])
+        bias_g_ps = psum_xgb.tile([P, HID], F32, name="xgb")
+        nc.tensor.matmul(out=bias_g_ps[:], lhsT=ones[:], rhs=bias_row[:, PEEPHOLES * HID :], start=True, stop=True)
+        bias_g = const.tile([P, HID], F32)
+        nc.scalar.copy(out=bias_g[:], in_=bias_g_ps[:])
+        bias_f = const.tile([P, HID], BF16)
+        nc.scalar.copy(out=bias_f[:], in_=bias_if[:, HID : 2 * HID])
         ident_bf = const.tile([P, P], BF16)
         make_identity(nc, ident_bf[:])
 
@@ -110,7 +111,7 @@ def tile_ircnn_lstmcell_pa_t_kernel(
             rows = slice(pair * PAIR, (pair + 1) * PAIR)
             hx_pair = loads.tile([P, PAIR, HID], BF16, bufs=STATES_AHEAD - 1)
             nc.sync.dma_start(out=hx_pair[:], in_=hx_v[:, rows, :])
-            cx_pair = loads.tile([P, PAIR, HID], BF16, bufs=STATES_AHEAD + 2)
+            cx_pair = loads.tile([P, PAIR, HID], BF16, bufs=5)
             nc.sync.dma_start(out=cx_pair[:], in_=cx_v[:, rows, :])
             hx_sb[pair] = hx_pair
             cx_sb[pair] = cx_pair
@@ -189,7 +190,7 @@ def tile_ircnn_lstmcell_pa_t_kernel(
 
         def regroup(t):
             if t % BATCH == 0:
-                quads = work.tile([P, BATCH, 2 * P * 4], BF16, align_bytes=64, bufs=2)
+                quads = work.tile([P, BATCH, 2 * P * 4], BF16, align_bytes=64, bufs=4)
                 grouped[t // BATCH] = quads
             nc.scalar.copy(
                 out=grouped[t // BATCH][:, t % BATCH, :]
@@ -234,8 +235,11 @@ def tile_ircnn_lstmcell_pa_t_kernel(
                     mx_pass(bank, t, 1, (GATES + gate) * HID, False, True)
                 acc[(t, gate)] = bank
 
+        def pe_pair(pair):
+            return pair >= 1 and pair % 4 != 0
+
         def by_pe(t, gate):
-            return gate == GATES - 1 and t >= 2 * PAIR and t % PAIR == 0
+            return gate == GATES - 1 and pe_pair(t // PAIR)
 
         xgb_bank = {}
 
@@ -254,40 +258,49 @@ def tile_ircnn_lstmcell_pa_t_kernel(
                     cols = slice(gate * HID, (gate + 1) * HID)
                     nc.scalar.copy(out=gates_sb[t // PAIR][:, t % PAIR, cols], in_=xgb_bank[(t, gate)][:])
 
+        def f_on_gpsimd(t):
+            return t % PAIR == 1
+
         def add_bias_f(pair):
             gates_pair = work.tile([P, PAIR, GATES * HID], F32, bufs=GATE_BUFS)
             gates_sb[pair] = gates_pair
-            nc.gpsimd.tensor_tensor(
-                out=gates_pair[:, :, HID : 2 * HID],
-                in0=xg_sb[pair][:, :, HID : 2 * HID],
-                in1=bias_f[:].unsqueeze(1).to_broadcast([P, PAIR, HID]),
-                op=ALU.add,
-            )
+            for j in range(PAIR):
+                if f_on_gpsimd(pair * PAIR + j):
+                    nc.gpsimd.tensor_tensor(
+                        out=gates_pair[:, j, HID : 2 * HID], in0=xg_sb[pair][:, j, HID : 2 * HID], in1=bias_f[:], op=ALU.add
+                    )
+            if not pe_pair(pair):
+                nc.gpsimd.tensor_tensor(
+                    out=gates_pair[:, :, PEEPHOLES * HID :],
+                    in0=xg_sb[pair][:, :, PEEPHOLES * HID :],
+                    in1=bias_g[:].unsqueeze(1).to_broadcast([P, PAIR, HID]),
+                    op=ALU.add,
+                )
 
         cx_bank = {}
 
         def cx_to_psum(t):
-            bank = psum_cx.tile([P, HID], F32)
-            nc.tensor.matmul(out=bank[:], lhsT=ident_bf[:], rhs=cx_sb[t // PAIR][:, t % PAIR, :], start=True, stop=True)
+            bank = psum_cx.tile([P, P, 2], F32)
+            words = grouped[t // BATCH][:, t % BATCH, :].bitcast(F32)[:, 2 * P : 4 * P].rearrange("p (r u) -> p r u", u=2)
+            for u in range(2):
+                nc.tensor.transpose(bank[:, :, u], words[:, :, u], ident[:])
             cx_bank[t] = bank
 
         def forget_term(t):
             f_g = gates_sb[t // PAIR][:, t % PAIR, HID : 2 * HID]
+            cx_rows = cx_bank[t][:].rearrange("r p u -> r (p u)").bitcast(BF16)
             nc.vector.scalar_tensor_tensor(
-                out=f_g, in0=cx_bank[t][:], scalar=decay[:, 0, t : t + 1], in1=f_g, op0=ALU.mult, op1=ALU.mult
+                out=f_g, in0=cx_rows, scalar=decay[:, 0, t : t + 1], in1=f_g, op0=ALU.mult, op1=ALU.mult
             )
 
         def add_bias(t):
-            for gate in range(GATES):
-                if by_pe(t, gate) or gate == 1:
-                    continue
-                cols = slice(gate * HID, (gate + 1) * HID)
-                nc.vector.tensor_tensor(
-                    out=gates_sb[t // PAIR][:, t % PAIR, cols],
-                    in0=xg_sb[t // PAIR][:, t % PAIR, cols],
-                    in1=bias_bank[gate],
-                    op=ALU.add,
-                )
+            cols = slice(0, HID if f_on_gpsimd(t) else PEEPHOLES * HID)
+            nc.vector.tensor_tensor(
+                out=gates_sb[t // PAIR][:, t % PAIR, cols],
+                in0=xg_sb[t // PAIR][:, t % PAIR, cols],
+                in1=bias_if[:, cols],
+                op=ALU.add,
+            )
 
         def add_products(t):
             for gate in range(GATES):

from contextlib import ExitStack

import concourse.mybir as mybir
from concourse.masks import make_identity

F32 = mybir.dt.float32
BF16 = mybir.dt.bfloat16
I32 = mybir.dt.int32
U32 = mybir.dt.uint32
U8 = mybir.dt.uint8
FP8X4 = mybir.dt.float8_e4m3fn_x4
ACT = mybir.ActivationFunctionType
ALU = mybir.AluOpType

P = 128
ROWS = 4096
HID = 512
GATES = 3
PEEPHOLES = 2
TILES = ROWS // P
PAIR = 2
PAIRS = TILES // PAIR
WORDS = HID // 2
W_COLS = (GATES + PEEPHOLES) * HID
BATCH = 4
STATES_AHEAD = 5
XG_AHEAD = 4
F_AHEAD = 3
GATE_BUFS = 6
TAIL_PAIRS = 2

FLOPS = 2 * ROWS * HID * W_COLS


def tile_ircnn_lstmcell_pa_t_kernel(
    tc,
    xg,
    hx,
    cx,
    td0,
    td1,
    w_hh_words,
    w_hh_scales,
    w_pi_words,
    w_pi_scales,
    w_pf_words,
    w_pf_scales,
    b_hh,
    a,
    b,
    out,
):
    nc = tc.nc

    xg_v = xg.rearrange("(p t) c -> p t c", t=TILES)
    hx_v = hx.rearrange("(p t) c -> p t c", t=TILES)
    cx_v = cx.rearrange("(p t) c -> p t c", t=TILES)
    out_v = out.rearrange("(p t) c -> p t c", t=TILES)

    with ExitStack() as ctx:
        const = ctx.enter_context(tc.tile_pool(name="const", bufs=1))
        loads = ctx.enter_context(tc.tile_pool(name="loads", bufs=1))
        work = ctx.enter_context(tc.tile_pool(name="work", bufs=1))
        psum_bias = ctx.enter_context(tc.psum_pool(name="psum_bias", bufs=1))
        psum_xt = ctx.enter_context(tc.psum_pool(name="psum_xt", bufs=2))
        psum_xgb = ctx.enter_context(tc.psum_pool(name="psum_xgb", bufs=1))
        psum_cx = ctx.enter_context(tc.psum_pool(name="psum_cx", bufs=1))
        psum_acc = ctx.enter_context(tc.psum_pool(name="psum_acc", bufs=3))
        ctx.enter_context(tc.manual_schedule())

        w_codes = const.tile([P, W_COLS], U32, align_bytes=64)
        w_scales = const.tile([P, W_COLS], U8, align_bytes=64)
        nc.vector.memset(w_scales[:].bitcast(I32), 0)
        weights = (
            (w_hh_words, w_hh_scales, 0, GATES * HID),
            (w_pi_words, w_pi_scales, GATES * HID, HID),
            (w_pf_words, w_pf_scales, GATES * HID + HID, HID),
        )

        bias_row = const.tile([P, GATES * HID], BF16)
        nc.vector.memset(bias_row[:], 0.0)
        nc.sync.dma_start(out=bias_row[0:1, :], in_=b_hh.rearrange("(o c) -> o c", o=1))
        ones = const.tile([P, P], BF16)
        nc.vector.memset(ones[:], 1.0)
        bias_if = psum_bias.tile([P, PEEPHOLES * HID], BF16, name="bias_if")
        for gate in range(PEEPHOLES):
            nc.tensor.matmul(
                out=bias_if[:, gate * HID : (gate + 1) * HID],
                lhsT=ones[:],
                rhs=bias_row[:, gate * HID : (gate + 1) * HID],
                start=True,
                stop=True,
            )
        bias_g_ps = psum_xgb.tile([P, HID], F32, name="xgb")
        nc.tensor.matmul(out=bias_g_ps[:], lhsT=ones[:], rhs=bias_row[:, PEEPHOLES * HID :], start=True, stop=True)
        bias_g = const.tile([P, HID], F32)
        nc.scalar.copy(out=bias_g[:], in_=bias_g_ps[:])
        bias_f = const.tile([P, HID], BF16)
        nc.scalar.copy(out=bias_f[:], in_=bias_if[:, HID : 2 * HID])
        ident_bf = const.tile([P, P], BF16)
        make_identity(nc, ident_bf[:])

        ident = const.tile([P, P], F32)
        make_identity(nc, ident[:])

        xg_sb = {}
        hx_sb = {}
        cx_sb = {}

        def load_states(pair):
            rows = slice(pair * PAIR, (pair + 1) * PAIR)
            hx_pair = loads.tile([P, PAIR, HID], BF16, bufs=STATES_AHEAD - 1)
            nc.sync.dma_start(out=hx_pair[:], in_=hx_v[:, rows, :])
            cx_pair = loads.tile([P, PAIR, HID], BF16, bufs=5)
            nc.sync.dma_start(out=cx_pair[:], in_=cx_v[:, rows, :])
            hx_sb[pair] = hx_pair
            cx_sb[pair] = cx_pair

        def load_xg(pair):
            rows = slice(pair * PAIR, (pair + 1) * PAIR)
            xg_pair = loads.tile([P, PAIR, GATES * HID], BF16, bufs=XG_AHEAD + 2)
            nc.sync.dma_start(out=xg_pair[:], in_=xg_v[:, rows, :])
            xg_sb[pair] = xg_pair

        def load_scales(which):
            words, scale_rows, first, width = weights[which]
            for quad in range(4):
                nc.sync.dma_start(
                    out=w_scales[32 * quad : 32 * quad + 4, first : first + width].bitcast(I32),
                    in_=scale_rows[0, 4 * quad : 4 * quad + 4, :].bitcast(I32),
                )

        def load_codes(which):
            words, scale_rows, first, width = weights[which]
            nc.sync.dma_start(
                out=w_codes[:, first : first + width].bitcast(I32),
                in_=words[0].rearrange("p n t -> p (n t)").bitcast(I32),
            )

        a_bf = const.tile([P, 1], BF16)
        b_bf = const.tile([P, 1], BF16)
        td_sb = const.tile([P, 2, TILES], BF16)
        decay = const.tile([P, 2, TILES], F32)

        def load_decay_inputs():
            nc.sync.dma_start(out=a_bf[:], in_=a.partition_broadcast(P))
            nc.sync.dma_start(out=b_bf[:], in_=b.partition_broadcast(P))
            nc.sync.dma_start(out=td_sb[:, 0, :], in_=td0.rearrange("(p t) -> p t", t=TILES))
            nc.sync.dma_start(out=td_sb[:, 1, :], in_=td1.rearrange("(p t) -> p t", t=TILES))

        def make_decay():
            a_f32 = const.tile([P, 1], F32)
            nc.scalar.copy(out=a_f32[:], in_=a_bf[:])
            minus_b = const.tile([P, 1], F32)
            nc.scalar.mul(out=minus_b[:], in_=b_bf[:], mul=-1.0)
            nc.scalar.activation(out=decay[:], in_=td_sb[:], func=ACT.Exp, scale=minus_b[:, 0:1])
            nc.scalar.activation(out=decay[:], in_=decay[:], func=ACT.Copy, scale=a_f32[:, 0:1])
            warm = const.tile([P, 1], F32)
            nc.scalar.activation(out=warm[:], in_=a_f32[:], func=ACT.Sigmoid)

        load_scales(0)
        load_states(0)
        load_codes(0)
        load_codes(1)
        load_scales(1)
        load_xg(0)
        load_decay_inputs()
        load_codes(2)
        load_scales(2)
        load_states(1)
        load_xg(1)
        load_states(2)
        load_states(3)
        load_xg(2)

        xt_bank = {}
        grouped = {}
        x_codes = {}
        x_scales = {}
        acc = {}
        gates_sb = {}

        def transpose(t):
            xt = psum_xt.tile([P, 2, 2, P], F32)
            for which, src in enumerate((hx_sb, cx_sb)):
                row_words = src[t // PAIR][:, t % PAIR, :].bitcast(F32)
                for u in range(2):
                    nc.tensor.transpose(xt[:, which, u, :], row_words[:, u:WORDS:2], ident[:])
            xt_bank[t] = xt

        def regroup(t):
            if t % BATCH == 0:
                quads = work.tile([P, BATCH, 2 * P * 4], BF16, align_bytes=64, bufs=4)
                grouped[t // BATCH] = quads
            nc.scalar.copy(
                out=grouped[t // BATCH][:, t % BATCH, :]
                .bitcast(F32)
                .rearrange("p (w r u) -> p w r u", w=2, u=2),
                in_=xt_bank[t][:].rearrange("p w u r -> p w r u"),
            )

        def quantise(batch, first_tile=0, tiles=BATCH):
            if first_tile == 0:
                codes = work.tile([P, BATCH * 2 * P], U32, align_bytes=64, bufs=2)
                plane = work.tile([P, BATCH * 2 * P], U8, align_bytes=64, bufs=2)
                x_codes[batch] = codes
                x_scales[batch] = plane
            cols = slice(first_tile * 2 * P, (first_tile + tiles) * 2 * P)
            nc.vector.quantize_mx(
                out=x_codes[batch][:, cols].bitcast(FP8X4),
                scales=x_scales[batch][:, cols],
                in_=grouped[batch][:, first_tile : first_tile + tiles, :].rearrange("p j c -> p (j c)"),
            )

        def mx_pass(bank, t, which, w_first, start, stop):
            first_row = ((t % BATCH) * 2 + which) * P
            rows = slice(first_row, first_row + P)
            cols = slice(w_first, w_first + HID)
            nc.tensor.matmul_mx(
                out=bank[:],
                lhsT=x_codes[t // BATCH][:, rows].bitcast(FP8X4),
                lhsT_scale=x_scales[t // BATCH][:, rows],
                rhs=w_codes[:, cols].bitcast(FP8X4),
                rhs_scale=w_scales[:, cols],
                start=start,
                stop=stop,
            )

        def matmuls(t):
            for gate in range(GATES):
                bank = psum_acc.tile([P, HID], F32)
                peephole = gate < PEEPHOLES
                mx_pass(bank, t, 0, gate * HID, True, not peephole)
                if peephole:
                    mx_pass(bank, t, 1, (GATES + gate) * HID, False, True)
                acc[(t, gate)] = bank

        def pe_pair(pair):
            return pair >= 1 and pair % 4 != 0

        def by_pe(t, gate):
            return gate == GATES - 1 and pe_pair(t // PAIR)

        xgb_bank = {}

        def pe_bias(t):
            for gate in range(GATES):
                if by_pe(t, gate):
                    cols = slice(gate * HID, (gate + 1) * HID)
                    bank = psum_xgb.tile([P, HID], F32, name="xgb")
                    nc.tensor.matmul(out=bank[:], lhsT=ident_bf[:], rhs=xg_sb[t // PAIR][:, t % PAIR, cols], start=True, stop=False)
                    nc.tensor.matmul(out=bank[:], lhsT=ones[:], rhs=bias_row[:, cols], start=False, stop=True)
                    xgb_bank[(t, gate)] = bank

        def copy_bias(t):
            for gate in range(GATES):
                if by_pe(t, gate):
                    cols = slice(gate * HID, (gate + 1) * HID)
                    nc.scalar.copy(out=gates_sb[t // PAIR][:, t % PAIR, cols], in_=xgb_bank[(t, gate)][:])

        def f_on_gpsimd(t):
            return t % PAIR == 1

        def add_bias_f(pair):
            gates_pair = work.tile([P, PAIR, GATES * HID], F32, bufs=GATE_BUFS)
            gates_sb[pair] = gates_pair
            for j in range(PAIR):
                if f_on_gpsimd(pair * PAIR + j):
                    nc.gpsimd.tensor_tensor(
                        out=gates_pair[:, j, HID : 2 * HID], in0=xg_sb[pair][:, j, HID : 2 * HID], in1=bias_f[:], op=ALU.add
                    )
            if not pe_pair(pair):
                nc.gpsimd.tensor_tensor(
                    out=gates_pair[:, :, PEEPHOLES * HID :],
                    in0=xg_sb[pair][:, :, PEEPHOLES * HID :],
                    in1=bias_g[:].unsqueeze(1).to_broadcast([P, PAIR, HID]),
                    op=ALU.add,
                )

        cx_bank = {}

        def cx_to_psum(t):
            bank = psum_cx.tile([P, P, 2], F32)
            words = grouped[t // BATCH][:, t % BATCH, :].bitcast(F32)[:, 2 * P : 4 * P].rearrange("p (r u) -> p r u", u=2)
            for u in range(2):
                nc.tensor.transpose(bank[:, :, u], words[:, :, u], ident[:])
            cx_bank[t] = bank

        def forget_term(t):
            f_g = gates_sb[t // PAIR][:, t % PAIR, HID : 2 * HID]
            cx_rows = cx_bank[t][:].rearrange("r p u -> r (p u)").bitcast(BF16)
            nc.vector.scalar_tensor_tensor(
                out=f_g, in0=cx_rows, scalar=decay[:, 0, t : t + 1], in1=f_g, op0=ALU.mult, op1=ALU.mult
            )

        def add_bias(t):
            cols = slice(0, HID if f_on_gpsimd(t) else PEEPHOLES * HID)
            nc.vector.tensor_tensor(
                out=gates_sb[t // PAIR][:, t % PAIR, cols],
                in0=xg_sb[t // PAIR][:, t % PAIR, cols],
                in1=bias_if[:, cols],
                op=ALU.add,
            )

        def add_products(t):
            for gate in range(GATES):
                cols = slice(gate * HID, (gate + 1) * HID)
                nc.vector.tensor_tensor(
                    out=gates_sb[t // PAIR][:, t % PAIR, cols],
                    in0=acc[(t, gate)][:],
                    in1=gates_sb[t // PAIR][:, t % PAIR, cols],
                    op=ALU.add,
                )

        def activate(t):
            mine = gates_sb[t // PAIR][:, t % PAIR, :]
            nc.scalar.activation(out=mine[:, 0 : 2 * HID], in_=mine[:, 0 : 2 * HID], func=ACT.Sigmoid)
            nc.scalar.activation(out=mine[:, 2 * HID :], in_=mine[:, 2 * HID :], func=ACT.Tanh)

        def scale_g(t):
            g_g = gates_sb[t // PAIR][:, t % PAIR, 2 * HID :]
            nc.scalar.activation(out=g_g, in_=g_g, func=ACT.Copy, scale=decay[:, 1, t : t + 1])

        def combine(pair):
            acts = gates_sb[pair]
            i_g = acts[:, :, 0:HID]
            f_g = acts[:, :, HID : 2 * HID]
            g_g = acts[:, :, 2 * HID :]
            new_c = work.tile([P, PAIR, HID], F32, bufs=3)
            nc.gpsimd.tensor_tensor(out=i_g, in0=i_g, in1=g_g, op=ALU.mult)
            nc.gpsimd.tensor_tensor(out=new_c[:], in0=i_g, in1=f_g, op=ALU.add)
            nc.sync.dma_start(out=out_v[:, pair * PAIR : (pair + 1) * PAIR, :], in_=new_c[:])

        tail_c = {}

        def combine_on_vector(t):
            if t % PAIR == 0:
                tail_pair = work.tile([P, PAIR, HID], F32, bufs=2)
                tail_c[t // PAIR] = tail_pair
            mine = gates_sb[t // PAIR][:, t % PAIR, :]
            i_g = mine[:, 0:HID]
            f_g = mine[:, HID : 2 * HID]
            g_g = mine[:, 2 * HID :]
            nc.vector.scalar_tensor_tensor(
                out=i_g, in0=i_g, scalar=decay[:, 1, t : t + 1], in1=g_g, op0=ALU.mult, op1=ALU.mult
            )
            nc.vector.tensor_tensor(out=tail_c[t // PAIR][:, t % PAIR, :], in0=i_g, in1=f_g, op=ALU.add)
            if t % PAIR == PAIR - 1:
                rows = slice(t + 1 - PAIR, t + 1)
                nc.sync.dma_start(out=out_v[:, rows, :], in_=tail_c[t // PAIR][:])

        def live(t):
            return 0 <= t < TILES

        def in_tail(t):
            return t // PAIR >= PAIRS - TAIL_PAIRS

        def to_transpose(t):
            return (2 * t + 4, 2 * t + 5) if t < 3 else (t + 7,)

        def to_regroup(t):
            return (2 * t + 2, 2 * t + 3) if t < 4 else (t + 6,)

        for t in range(-2, TILES):
            if t % PAIR == 0 and t // PAIR + STATES_AHEAD < PAIRS:
                load_states(t // PAIR + STATES_AHEAD)
            if t % PAIR == 0 and t // PAIR + XG_AHEAD < PAIRS:
                load_xg(t // PAIR + XG_AHEAD)
            for x in to_regroup(t):
                if live(x):
                    regroup(x)
            if t == -1:
                for pair in range(F_AHEAD):
                    add_bias_f(pair)
                make_decay()
                quantise(0, 0, PAIR)
                add_bias(0)
                pe_bias(0)
                copy_bias(0)
                add_bias(1)
                pe_bias(1)
                copy_bias(1)
            if live(t):
                add_products(t)
            if live(t + 1):
                matmuls(t + 1)

            for x in to_transpose(t):
                if live(x):
                    transpose(x)
            if live(t):
                activate(t)
            if live(t) and not in_tail(t):
                scale_g(t)
            if t == 0:
                add_bias(2)
                pe_bias(2)
                copy_bias(2)
                quantise(0, PAIR, PAIR)
            if t == 1:
                add_bias(3)
                pe_bias(3)
                copy_bias(3)
            if t == 2:
                add_bias(4)
                pe_bias(4)
                copy_bias(4)
            if t >= 2 and live(t + 3):
                add_bias(t + 3)
                pe_bias(t + 3)
                copy_bias(t + 3)
            if t >= 2 and live(t + 5) and (t + 5) % BATCH == BATCH - 1:
                quantise((t + 5) // BATCH)
            if live(t - 1):
                forget_term(t - 1)
            if live(t):
                cx_to_psum(t)
            if t % PAIR == 0 and live(t - PAIR) and not in_tail(t - PAIR):
                combine((t - PAIR) // PAIR)
            if t % PAIR == 0 and t >= 0 and t // PAIR + F_AHEAD < PAIRS:
                add_bias_f(t // PAIR + F_AHEAD)
        forget_term(TILES - 1)
        for t in range(TILES - TAIL_PAIRS * PAIR, TILES):
            combine_on_vector(t)
